import numpy as np
import ml_dtypes

BF16 = ml_dtypes.bfloat16


def bf(x):
    return np.asarray(x, np.float32).astype(BF16)


def f32(x):
    return np.asarray(x, np.float32)


def f64(x):
    return np.asarray(x).astype(np.float64)


def striped(idx):
    return np.tile(idx.reshape(-1, 16).T, (8, 1))


S, D, M, E, N = 4096, 128, 128, 2048, 4096
B2 = 0.25


def setup_inputs():
    return {
        "table": bf(np.random.standard_normal((D, S))),
        "w_src": bf(np.random.standard_normal((D, M)) / np.sqrt(D + D)),
        "w_dst": bf(np.random.standard_normal((D, M)) / np.sqrt(D + D)),
        "b1": f32(0.2 * np.random.standard_normal((M, 1))),
        "w2": bf(np.random.standard_normal((M, 1)) / np.sqrt(M)),
        "u1": f32(0.1 + 0.8 * np.random.random((1, E))),
        "u2": f32(0.1 + 0.8 * np.random.random((1, E))),
        "offs": striped(np.random.permutation(np.tile(np.arange(S), 2))[:N]),
    }


def reference(table, w_src, w_dst, b1, w2, u1, u2, offs):
    idx = offs[:16].T.reshape(-1)
    src, dst = idx[:E], idx[E:]
    t = f64(table)
    h = np.maximum(f64(w_src).T @ t[:, src] + f64(w_dst).T @ t[:, dst] + f64(b1), 0.0)
    logit = f64(w2).T @ h + B2
    n1 = -np.log(-np.log(f64(u1)))
    n2 = -np.log(-np.log(f64(u2)))
    return 1.0 / (1.0 + np.exp(-(logit + n1 - n2)))

@@ -1,0 +1,88 @@
+import concourse.mybir as mybir
+
+BF16, F32, U16 = mybir.dt.bfloat16, mybir.dt.float32, mybir.dt.uint16
+ACT = mybir.ActivationFunctionType
+ALU = mybir.AluOpType
+
+P = 128
+NODES = 4096
+EDGES = 2048
+PIECE = 512
+PIECES = EDGES // PIECE
+BLOCK = 128
+BLOCKS = EDGES // BLOCK
+BLOCKS_IN_PIECE = PIECE // BLOCK
+B2 = 0.25
+
+FLOPS = 2 * P * P * 2 * EDGES + 2 * P * EDGES
+
+
+def tile_learnable_edge_pruning_kernel(tc, table, w_src, w_dst, b1, w2, u1, u2, offs, out):
+    nc = tc.nc
+    with (
+        tc.tile_pool(name="held", bufs=1) as held,
+        tc.tile_pool(name="hidden", bufs=PIECES) as hidden,
+        tc.psum_pool(name="banks", bufs=PIECES) as banks,
+        tc.psum_pool(name="score", bufs=1) as score,
+    ):
+        offsets = held.tile([P, 2 * EDGES // 16], U16, name="offsets")
+        nc.sync.dma_start(offsets[:], offs)
+        nodes = held.tile([P, NODES], BF16, name="nodes")
+        nc.sync.dma_start(nodes[:], table)
+
+        draws = held.tile([BLOCKS, 2 * BLOCK], F32, name="draws")
+        nc.scalar.dma_start(draws[:, 0:BLOCK], u1.rearrange("o (s c) -> (o s) c", c=BLOCK))
+        nc.scalar.dma_start(draws[:, BLOCK : 2 * BLOCK], u2.rearrange("o (s c) -> (o s) c", c=BLOCK))
+        proj_src = held.tile([P, P], BF16, name="proj_src")
+        nc.scalar.dma_start(proj_src[:], w_src)
+        proj_dst = held.tile([P, P], BF16, name="proj_dst")
+        nc.scalar.dma_start(proj_dst[:], w_dst)
+        bias1 = held.tile([P, 1], F32, name="bias1")
+        nc.gpsimd.dma_start(bias1[:], b1)
+
+        w2_shift = held.tile([P, 2 * P - 1], BF16, name="w2_shift")
+        nc.vector.memset(w2_shift[:], 0.0)
+        nc.gpsimd.dma_start(w2_shift[:, P - 1 : P], w2)
+
+        logs = held.tile([BLOCKS, 2 * BLOCK], F32, name="logs")
+        nc.scalar.activation(logs[:], draws[:], ACT.Ln)
+        loglogs = held.tile([BLOCKS, 2 * BLOCK], F32, name="loglogs")
+        nc.scalar.activation(loglogs[:], logs[:], ACT.Ln, scale=-1.0)
+        noise = held.tile([BLOCKS, BLOCK], F32, name="noise")
+        nc.vector.tensor_sub(noise[:], loglogs[:, BLOCK : 2 * BLOCK], loglogs[:, 0:BLOCK])
+
+        logits = score.tile([P, BLOCK], F32, name="logits")
+
+        def first_layer(q):
+            bank = banks.tile([P, PIECE], F32, name="bank")
+            src_col = q * PIECE // 16
+            dst_col = (EDGES + q * PIECE) // 16
+            nc.tensor.matmul(
+                bank[:], proj_src[:], nodes[:].indirect(offsets[:, src_col : src_col + PIECE // 16]),
+                start=True, stop=False,
+            )
+            nc.tensor.matmul(
+                bank[:], proj_dst[:], nodes[:].indirect(offsets[:, dst_col : dst_col + PIECE // 16]),
+                start=False, stop=True,
+            )
+            h = hidden.tile([P, PIECE], BF16, name="h")
+            nc.vector.tensor_scalar(h[:], bank[:], bias1[:, 0:1], 0.0, op0=ALU.add, op1=ALU.max)
+            return h
+
+        def second_layer(q, h):
+            for k in range(BLOCKS_IN_PIECE):
+                s = q * BLOCKS_IN_PIECE + k
+                nc.tensor.matmul(
+                    logits[:], w2_shift[:, P - 1 - s : 2 * P - 1 - s], h[:, k * BLOCK : (k + 1) * BLOCK],
+                    start=(s == 0), stop=(s == BLOCKS - 1),
+                )
+
+        h_of = [first_layer(q) for q in range(PIECES)]
+        for q in range(PIECES):
+            second_layer(q, h_of[q])
+
+        noisy = held.tile([BLOCKS, BLOCK], F32, name="noisy")
+        nc.vector.tensor_tensor(noisy[:], logits[0:BLOCKS, :], noise[:], ALU.add)
+        keep = held.tile([BLOCKS, BLOCK], F32, name="keep")
+        nc.scalar.activation(keep[:], noisy[:], ACT.Sigmoid, bias=B2)
+        nc.sync.dma_start(out.rearrange("o (s c) -> (o s) c", c=BLOCK), keep[:])

@@ -1,3 +1,4 @@
+import concourse.masks as masks
 import concourse.mybir as mybir
 
 BF16, F32, U16 = mybir.dt.bfloat16, mybir.dt.float32, mybir.dt.uint16
@@ -13,6 +14,7 @@ BLOCK = 128
 BLOCKS = EDGES // BLOCK
 BLOCKS_IN_PIECE = PIECE // BLOCK
 B2 = 0.25
+WARM_UP = 10
 
 FLOPS = 2 * P * P * 2 * EDGES + 2 * P * EDGES
 
@@ -25,25 +27,34 @@ def tile_learnable_edge_pruning_kernel(tc, table, w_src, w_dst, b1, w2, u1, u2, 
         tc.psum_pool(name="banks", bufs=PIECES) as banks,
         tc.psum_pool(name="score", bufs=1) as score,
     ):
-        offsets = held.tile([P, 2 * EDGES // 16], U16, name="offsets")
-        nc.sync.dma_start(offsets[:], offs)
-        nodes = held.tile([P, NODES], BF16, name="nodes")
-        nc.sync.dma_start(nodes[:], table)
-
         draws = held.tile([BLOCKS, 2 * BLOCK], F32, name="draws")
         nc.scalar.dma_start(draws[:, 0:BLOCK], u1.rearrange("o (s c) -> (o s) c", c=BLOCK))
         nc.scalar.dma_start(draws[:, BLOCK : 2 * BLOCK], u2.rearrange("o (s c) -> (o s) c", c=BLOCK))
+        offsets = held.tile([P, 2 * EDGES // 16], U16, name="offsets")
+        nc.sync.dma_start(offsets[:], offs)
+        nodes = held.tile([P, NODES], BF16, name="nodes")
+        nc.sync.dma_start(nodes[:, 0 : NODES // 2], table[:, 0 : NODES // 2])
+        nc.scalar.dma_start(nodes[:, NODES // 2 : NODES], table[:, NODES // 2 : NODES])
         proj_src = held.tile([P, P], BF16, name="proj_src")
         nc.scalar.dma_start(proj_src[:], w_src)
         proj_dst = held.tile([P, P], BF16, name="proj_dst")
         nc.scalar.dma_start(proj_dst[:], w_dst)
         bias1 = held.tile([P, 1], F32, name="bias1")
-        nc.gpsimd.dma_start(bias1[:], b1)
+        nc.scalar.dma_start(bias1[:], b1)
 
         w2_shift = held.tile([P, 2 * P - 1], BF16, name="w2_shift")
         nc.vector.memset(w2_shift[:], 0.0)
-        nc.gpsimd.dma_start(w2_shift[:, P - 1 : P], w2)
+        nc.sync.dma_start(w2_shift[:, P - 1 : P], w2)
 
+        zeros = held.tile([P, PIECE], BF16, name="zeros")
+        nc.vector.memset(zeros[:], 0.0)
+        idle_bank = score.tile([P, PIECE], F32, name="idle_bank")
+        for i in range(WARM_UP):
+            nc.tensor.matmul(idle_bank[:], zeros[:, 0:P], zeros[:], start=True, stop=True)
+
+        one = held.tile([P, 1], F32, name="one")
+        nc.vector.memset(one[:], 1.0)
+        nc.scalar.activation(one[:], one[:], ACT.Ln)
         logs = held.tile([BLOCKS, 2 * BLOCK], F32, name="logs")
         nc.scalar.activation(logs[:], draws[:], ACT.Ln)
         loglogs = held.tile([BLOCKS, 2 * BLOCK], F32, name="loglogs")
@@ -52,6 +63,9 @@ def tile_learnable_edge_pruning_kernel(tc, table, w_src, w_dst, b1, w2, u1, u2, 
         nc.vector.tensor_sub(noise[:], loglogs[:, BLOCK : 2 * BLOCK], loglogs[:, 0:BLOCK])
 
         logits = score.tile([P, BLOCK], F32, name="logits")
+        identity = held.tile([P, P], F32, name="identity")
+        masks.make_identity(nc, identity[:])
+        nc.tensor.matmul(logits[:], identity[0:BLOCKS, :], noise[:], start=True, stop=False)
 
         def first_layer(q):
             bank = banks.tile([P, PIECE], F32, name="bank")
@@ -74,15 +88,13 @@ def tile_learnable_edge_pruning_kernel(tc, table, w_src, w_dst, b1, w2, u1, u2, 
                 s = q * BLOCKS_IN_PIECE + k
                 nc.tensor.matmul(
                     logits[:], w2_shift[:, P - 1 - s : 2 * P - 1 - s], h[:, k * BLOCK : (k + 1) * BLOCK],
-                    start=(s == 0), stop=(s == BLOCKS - 1),
+                    start=False, stop=(s == BLOCKS - 1),
                 )
 
         h_of = [first_layer(q) for q in range(PIECES)]
         for q in range(PIECES):
             second_layer(q, h_of[q])
 
-        noisy = held.tile([BLOCKS, BLOCK], F32, name="noisy")
-        nc.vector.tensor_tensor(noisy[:], logits[0:BLOCKS, :], noise[:], ALU.add)
         keep = held.tile([BLOCKS, BLOCK], F32, name="keep")
-        nc.scalar.activation(keep[:], noisy[:], ACT.Sigmoid, bias=B2)
+        nc.scalar.activation(keep[:], logits[0:BLOCKS, :], ACT.Sigmoid, bias=B2)
         nc.sync.dma_start(out.rearrange("o (s c) -> (o s) c", c=BLOCK), keep[:])

@@ -1,4 +1,3 @@
-import concourse.masks as masks
 import concourse.mybir as mybir
 
 BF16, F32, U16 = mybir.dt.bfloat16, mybir.dt.float32, mybir.dt.uint16
@@ -14,7 +13,7 @@ BLOCK = 128
 BLOCKS = EDGES // BLOCK
 BLOCKS_IN_PIECE = PIECE // BLOCK
 B2 = 0.25
-WARM_UP = 10
+WARM_UP = 6
 
 FLOPS = 2 * P * P * 2 * EDGES + 2 * P * EDGES
 
@@ -27,34 +26,31 @@ def tile_learnable_edge_pruning_kernel(tc, table, w_src, w_dst, b1, w2, u1, u2, 
         tc.psum_pool(name="banks", bufs=PIECES) as banks,
         tc.psum_pool(name="score", bufs=1) as score,
     ):
-        draws = held.tile([BLOCKS, 2 * BLOCK], F32, name="draws")
-        nc.scalar.dma_start(draws[:, 0:BLOCK], u1.rearrange("o (s c) -> (o s) c", c=BLOCK))
-        nc.scalar.dma_start(draws[:, BLOCK : 2 * BLOCK], u2.rearrange("o (s c) -> (o s) c", c=BLOCK))
+        zeros = held.tile([P, PIECE], BF16, name="zeros")
+        nc.gpsimd.memset(zeros[:], 0.0)
+        idle_bank = score.tile([P, PIECE], F32, name="idle_bank")
+        for i in range(WARM_UP):
+            nc.tensor.matmul(idle_bank[:], zeros[:, 0:P], zeros[:], start=True, stop=True)
+
         offsets = held.tile([P, 2 * EDGES // 16], U16, name="offsets")
         nc.sync.dma_start(offsets[:], offs)
         nodes = held.tile([P, NODES], BF16, name="nodes")
-        nc.sync.dma_start(nodes[:, 0 : NODES // 2], table[:, 0 : NODES // 2])
-        nc.scalar.dma_start(nodes[:, NODES // 2 : NODES], table[:, NODES // 2 : NODES])
+        nc.sync.dma_start(nodes[:], table)
+
+        draws = held.tile([BLOCKS, 2 * BLOCK], F32, name="draws")
+        nc.scalar.dma_start(draws[:, 0:BLOCK], u1.rearrange("o (s c) -> (o s) c", c=BLOCK))
+        nc.scalar.dma_start(draws[:, BLOCK : 2 * BLOCK], u2.rearrange("o (s c) -> (o s) c", c=BLOCK))
         proj_src = held.tile([P, P], BF16, name="proj_src")
         nc.scalar.dma_start(proj_src[:], w_src)
         proj_dst = held.tile([P, P], BF16, name="proj_dst")
         nc.scalar.dma_start(proj_dst[:], w_dst)
         bias1 = held.tile([P, 1], F32, name="bias1")
-        nc.scalar.dma_start(bias1[:], b1)
+        nc.gpsimd.dma_start(bias1[:], b1)
 
         w2_shift = held.tile([P, 2 * P - 1], BF16, name="w2_shift")
         nc.vector.memset(w2_shift[:], 0.0)
-        nc.sync.dma_start(w2_shift[:, P - 1 : P], w2)
+        nc.gpsimd.dma_start(w2_shift[:, P - 1 : P], w2)
 
-        zeros = held.tile([P, PIECE], BF16, name="zeros")
-        nc.vector.memset(zeros[:], 0.0)
-        idle_bank = score.tile([P, PIECE], F32, name="idle_bank")
-        for i in range(WARM_UP):
-            nc.tensor.matmul(idle_bank[:], zeros[:, 0:P], zeros[:], start=True, stop=True)
-
-        one = held.tile([P, 1], F32, name="one")
-        nc.vector.memset(one[:], 1.0)
-        nc.scalar.activation(one[:], one[:], ACT.Ln)
         logs = held.tile([BLOCKS, 2 * BLOCK], F32, name="logs")
         nc.scalar.activation(logs[:], draws[:], ACT.Ln)
         loglogs = held.tile([BLOCKS, 2 * BLOCK], F32, name="loglogs")
@@ -63,9 +59,6 @@ def tile_learnable_edge_pruning_kernel(tc, table, w_src, w_dst, b1, w2, u1, u2, 
         nc.vector.tensor_sub(noise[:], loglogs[:, BLOCK : 2 * BLOCK], loglogs[:, 0:BLOCK])
 
         logits = score.tile([P, BLOCK], F32, name="logits")
-        identity = held.tile([P, P], F32, name="identity")
-        masks.make_identity(nc, identity[:])
-        nc.tensor.matmul(logits[:], identity[0:BLOCKS, :], noise[:], start=True, stop=False)
 
         def first_layer(q):
             bank = banks.tile([P, PIECE], F32, name="bank")
@@ -88,13 +81,15 @@ def tile_learnable_edge_pruning_kernel(tc, table, w_src, w_dst, b1, w2, u1, u2, 
                 s = q * BLOCKS_IN_PIECE + k
                 nc.tensor.matmul(
                     logits[:], w2_shift[:, P - 1 - s : 2 * P - 1 - s], h[:, k * BLOCK : (k + 1) * BLOCK],
-                    start=False, stop=(s == BLOCKS - 1),
+                    start=(s == 0), stop=(s == BLOCKS - 1),
                 )
 
         h_of = [first_layer(q) for q in range(PIECES)]
         for q in range(PIECES):
             second_layer(q, h_of[q])
 
+        noisy = held.tile([BLOCKS, BLOCK], F32, name="noisy")
+        nc.vector.tensor_tensor(noisy[:], logits[0:BLOCKS, :], noise[:], ALU.add)
         keep = held.tile([BLOCKS, BLOCK], F32, name="keep")
-        nc.scalar.activation(keep[:], logits[0:BLOCKS, :], ACT.Sigmoid, bias=B2)
+        nc.scalar.activation(keep[:], noisy[:], ACT.Sigmoid, bias=B2)
         nc.sync.dma_start(out.rearrange("o (s c) -> (o s) c", c=BLOCK), keep[:])

@@ -47,9 +47,9 @@ def tile_learnable_edge_pruning_kernel(tc, table, w_src, w_dst, b1, w2, u1, u2, 
         bias1 = held.tile([P, 1], F32, name="bias1")
         nc.gpsimd.dma_start(bias1[:], b1)
 
-        w2_shift = held.tile([P, 2 * P - 1], BF16, name="w2_shift")
+        w2_shift = held.tile([P, 2 * P], BF16, name="w2_shift")
         nc.vector.memset(w2_shift[:], 0.0)
-        nc.gpsimd.dma_start(w2_shift[:, P - 1 : P], w2)
+        nc.gpsimd.dma_start(w2_shift[:, P : P + 1], w2)
 
         logs = held.tile([BLOCKS, 2 * BLOCK], F32, name="logs")
         nc.scalar.activation(logs[:], draws[:], ACT.Ln)
@@ -80,7 +80,7 @@ def tile_learnable_edge_pruning_kernel(tc, table, w_src, w_dst, b1, w2, u1, u2, 
             for k in range(BLOCKS_IN_PIECE):
                 s = q * BLOCKS_IN_PIECE + k
                 nc.tensor.matmul(
-                    logits[:], w2_shift[:, P - 1 - s : 2 * P - 1 - s], h[:, k * BLOCK : (k + 1) * BLOCK],
+                    logits[:], w2_shift[:, P - s : 2 * P - s], h[:, k * BLOCK : (k + 1) * BLOCK],
                     start=(s == 0), stop=(s == BLOCKS - 1),
                 )
 

@@ -10,12 +10,17 @@ EDGES = 2048
 PIECE = 512
 PIECES = EDGES // PIECE
 BLOCK = 128
-BLOCKS = EDGES // BLOCK
 BLOCKS_IN_PIECE = PIECE // BLOCK
+GROUP = 32
+ROW_STEP = GROUP // PIECES
 B2 = 0.25
 WARM_UP = 6
 
 FLOPS = 2 * P * P * 2 * EDGES + 2 * P * EDGES
+
+
+def by_block(row):
+    return row.rearrange("o (q k c) -> (o k) q c", q=PIECES, k=BLOCKS_IN_PIECE)
 
 
 def tile_learnable_edge_pruning_kernel(tc, table, w_src, w_dst, b1, w2, u1, u2, offs, out):
@@ -37,9 +42,10 @@ def tile_learnable_edge_pruning_kernel(tc, table, w_src, w_dst, b1, w2, u1, u2, 
         nodes = held.tile([P, NODES], BF16, name="nodes")
         nc.sync.dma_start(nodes[:], table)
 
-        draws = held.tile([BLOCKS, 2 * BLOCK], F32, name="draws")
-        nc.scalar.dma_start(draws[:, 0:BLOCK], u1.rearrange("o (s c) -> (o s) c", c=BLOCK))
-        nc.scalar.dma_start(draws[:, BLOCK : 2 * BLOCK], u2.rearrange("o (s c) -> (o s) c", c=BLOCK))
+        draws = held.tile([P, 2 * BLOCK], F32, name="draws")
+        nc.vector.memset(draws[:], 0.5)
+        nc.scalar.dma_start(draws[0:P:ROW_STEP, 0:BLOCK], by_block(u1))
+        nc.scalar.dma_start(draws[0:P:ROW_STEP, BLOCK : 2 * BLOCK], by_block(u2))
         proj_src = held.tile([P, P], BF16, name="proj_src")
         nc.scalar.dma_start(proj_src[:], w_src)
         proj_dst = held.tile([P, P], BF16, name="proj_dst")
@@ -47,15 +53,15 @@ def tile_learnable_edge_pruning_kernel(tc, table, w_src, w_dst, b1, w2, u1, u2, 
         bias1 = held.tile([P, 1], F32, name="bias1")
         nc.gpsimd.dma_start(bias1[:], b1)
 
-        w2_shift = held.tile([P, 2 * P], BF16, name="w2_shift")
+        w2_shift = held.tile([P, 2 * GROUP], BF16, name="w2_shift")
         nc.vector.memset(w2_shift[:], 0.0)
-        nc.gpsimd.dma_start(w2_shift[:, P : P + 1], w2)
+        nc.gpsimd.dma_start(w2_shift[:, GROUP : GROUP + 1], w2)
 
-        logs = held.tile([BLOCKS, 2 * BLOCK], F32, name="logs")
+        logs = held.tile([P, 2 * BLOCK], F32, name="logs")
         nc.scalar.activation(logs[:], draws[:], ACT.Ln)
-        loglogs = held.tile([BLOCKS, 2 * BLOCK], F32, name="loglogs")
+        loglogs = held.tile([P, 2 * BLOCK], F32, name="loglogs")
         nc.scalar.activation(loglogs[:], logs[:], ACT.Ln, scale=-1.0)
-        noise = held.tile([BLOCKS, BLOCK], F32, name="noise")
+        noise = held.tile([P, BLOCK], F32, name="noise")
         nc.vector.tensor_sub(noise[:], loglogs[:, BLOCK : 2 * BLOCK], loglogs[:, 0:BLOCK])
 
         logits = score.tile([P, BLOCK], F32, name="logits")
@@ -77,19 +83,21 @@ def tile_learnable_edge_pruning_kernel(tc, table, w_src, w_dst, b1, w2, u1, u2, 
             return h
 
         def second_layer(q, h):
+            row = ROW_STEP * q
             for k in range(BLOCKS_IN_PIECE):
-                s = q * BLOCKS_IN_PIECE + k
                 nc.tensor.matmul(
-                    logits[:], w2_shift[:, P - s : 2 * P - s], h[:, k * BLOCK : (k + 1) * BLOCK],
-                    start=(s == 0), stop=(s == BLOCKS - 1),
+                    logits[GROUP * k : GROUP * (k + 1), :],
+                    w2_shift[:, GROUP - row : 2 * GROUP - row],
+                    h[:, k * BLOCK : (k + 1) * BLOCK],
+                    start=(q == 0), stop=(q == PIECES - 1),
                 )
 
         h_of = [first_layer(q) for q in range(PIECES)]
         for q in range(PIECES):
             second_layer(q, h_of[q])
 
-        noisy = held.tile([BLOCKS, BLOCK], F32, name="noisy")
-        nc.vector.tensor_tensor(noisy[:], logits[0:BLOCKS, :], noise[:], ALU.add)
-        keep = held.tile([BLOCKS, BLOCK], F32, name="keep")
+        noisy = held.tile([P, BLOCK], F32, name="noisy")
+        nc.vector.tensor_tensor(noisy[:], logits[:], noise[:], ALU.add)
+        keep = held.tile([P, BLOCK], F32, name="keep")
         nc.scalar.activation(keep[:], noisy[:], ACT.Sigmoid, bias=B2)
-        nc.sync.dma_start(out.rearrange("o (s c) -> (o s) c", c=BLOCK), keep[:])
+        nc.sync.dma_start(by_block(out), keep[0:P:ROW_STEP, :])

@@ -42,14 +42,15 @@ def tile_learnable_edge_pruning_kernel(tc, table, w_src, w_dst, b1, w2, u1, u2, 
         nodes = held.tile([P, NODES], BF16, name="nodes")
         nc.sync.dma_start(nodes[:], table)
 
-        draws = held.tile([P, 2 * BLOCK], F32, name="draws")
-        nc.vector.memset(draws[:], 0.5)
-        nc.scalar.dma_start(draws[0:P:ROW_STEP, 0:BLOCK], by_block(u1))
-        nc.scalar.dma_start(draws[0:P:ROW_STEP, BLOCK : 2 * BLOCK], by_block(u2))
         proj_src = held.tile([P, P], BF16, name="proj_src")
         nc.scalar.dma_start(proj_src[:], w_src)
         proj_dst = held.tile([P, P], BF16, name="proj_dst")
         nc.scalar.dma_start(proj_dst[:], w_dst)
+
+        draws = held.tile([P, 2 * BLOCK], F32, name="draws")
+        nc.vector.memset(draws[:], 0.5)
+        nc.scalar.dma_start(draws[0:P:ROW_STEP, 0:BLOCK], by_block(u1))
+        nc.scalar.dma_start(draws[0:P:ROW_STEP, BLOCK : 2 * BLOCK], by_block(u2))
         bias1 = held.tile([P, 1], F32, name="bias1")
         nc.gpsimd.dma_start(bias1[:], b1)
 

@@ -37,10 +37,10 @@ def tile_learnable_edge_pruning_kernel(tc, table, w_src, w_dst, b1, w2, u1, u2, 
         for i in range(WARM_UP):
             nc.tensor.matmul(idle_bank[:], zeros[:, 0:P], zeros[:], start=True, stop=True)
 
-        offsets = held.tile([P, 2 * EDGES // 16], U16, name="offsets")
-        nc.sync.dma_start(offsets[:], offs)
         nodes = held.tile([P, NODES], BF16, name="nodes")
         nc.sync.dma_start(nodes[:], table)
+        offsets = held.tile([P, 2 * EDGES // 16], U16, name="offsets")
+        nc.sync.dma_start(offsets[:], offs)
 
         proj_src = held.tile([P, P], BF16, name="proj_src")
         nc.scalar.dma_start(proj_src[:], w_src)

@@ -1,4 +1,5 @@
 import concourse.mybir as mybir
+from concourse.masks import make_identity
 
 BF16, F32, U16 = mybir.dt.bfloat16, mybir.dt.float32, mybir.dt.uint16
 ACT = mybir.ActivationFunctionType
@@ -65,6 +66,9 @@ def tile_learnable_edge_pruning_kernel(tc, table, w_src, w_dst, b1, w2, u1, u2, 
         noise = held.tile([P, BLOCK], F32, name="noise")
         nc.vector.tensor_sub(noise[:], loglogs[:, BLOCK : 2 * BLOCK], loglogs[:, 0:BLOCK])
 
+        identity = held.tile([P, P], F32, name="identity")
+        make_identity(nc, identity[:])
+
         logits = score.tile([P, BLOCK], F32, name="logits")
 
         def first_layer(q):
@@ -90,15 +94,14 @@ def tile_learnable_edge_pruning_kernel(tc, table, w_src, w_dst, b1, w2, u1, u2, 
                     logits[GROUP * k : GROUP * (k + 1), :],
                     w2_shift[:, GROUP - row : 2 * GROUP - row],
                     h[:, k * BLOCK : (k + 1) * BLOCK],
-                    start=(q == 0), stop=(q == PIECES - 1),
+                    start=False, stop=(q == PIECES - 1),
                 )
 
         h_of = [first_layer(q) for q in range(PIECES)]
+        nc.tensor.matmul(logits[:], identity[:], noise[:], start=True, stop=False)
         for q in range(PIECES):
             second_layer(q, h_of[q])
 
-        noisy = held.tile([P, BLOCK], F32, name="noisy")
-        nc.vector.tensor_tensor(noisy[:], logits[:], noise[:], ALU.add)
         keep = held.tile([P, BLOCK], F32, name="keep")
-        nc.scalar.activation(keep[:], noisy[:], ACT.Sigmoid, bias=B2)
+        nc.scalar.activation(keep[:], logits[:], ACT.Sigmoid, bias=B2)
         nc.sync.dma_start(by_block(out), keep[0:P:ROW_STEP, :])

@@ -15,7 +15,6 @@ BLOCKS_IN_PIECE = PIECE // BLOCK
 GROUP = 32
 ROW_STEP = GROUP // PIECES
 B2 = 0.25
-WARM_UP = 6
 
 FLOPS = 2 * P * P * 2 * EDGES + 2 * P * EDGES
 
@@ -32,12 +31,6 @@ def tile_learnable_edge_pruning_kernel(tc, table, w_src, w_dst, b1, w2, u1, u2, 
         tc.psum_pool(name="banks", bufs=PIECES) as banks,
         tc.psum_pool(name="score", bufs=1) as score,
     ):
-        zeros = held.tile([P, PIECE], BF16, name="zeros")
-        nc.gpsimd.memset(zeros[:], 0.0)
-        idle_bank = score.tile([P, PIECE], F32, name="idle_bank")
-        for i in range(WARM_UP):
-            nc.tensor.matmul(idle_bank[:], zeros[:, 0:P], zeros[:], start=True, stop=True)
-
         nodes = held.tile([P, NODES], BF16, name="nodes")
         nc.sync.dma_start(nodes[:], table)
         offsets = held.tile([P, 2 * EDGES // 16], U16, name="offsets")

@@ -32,14 +32,14 @@ def tile_learnable_edge_pruning_kernel(tc, table, w_src, w_dst, b1, w2, u1, u2, 
         tc.psum_pool(name="score", bufs=1) as score,
     ):
         nodes = held.tile([P, NODES], BF16, name="nodes")
-        nc.sync.dma_start(nodes[:], table)
-        offsets = held.tile([P, 2 * EDGES // 16], U16, name="offsets")
-        nc.sync.dma_start(offsets[:], offs)
+        nc.scalar.dma_start(nodes[:], table)
 
         proj_src = held.tile([P, P], BF16, name="proj_src")
-        nc.scalar.dma_start(proj_src[:], w_src)
+        nc.sync.dma_start(proj_src[:], w_src)
         proj_dst = held.tile([P, P], BF16, name="proj_dst")
-        nc.scalar.dma_start(proj_dst[:], w_dst)
+        nc.sync.dma_start(proj_dst[:], w_dst)
+        offsets = held.tile([P, 2 * EDGES // 16], U16, name="offsets")
+        nc.sync.dma_start(offsets[:], offs)
 
         draws = held.tile([P, 2 * BLOCK], F32, name="draws")
         nc.vector.memset(draws[:], 0.5)
@@ -57,7 +57,7 @@ def tile_learnable_edge_pruning_kernel(tc, table, w_src, w_dst, b1, w2, u1, u2, 
         loglogs = held.tile([P, 2 * BLOCK], F32, name="loglogs")
         nc.scalar.activation(loglogs[:], logs[:], ACT.Ln, scale=-1.0)
         noise = held.tile([P, BLOCK], F32, name="noise")
-        nc.vector.tensor_sub(noise[:], loglogs[:, BLOCK : 2 * BLOCK], loglogs[:, 0:BLOCK])
+        nc.gpsimd.tensor_sub(noise[:], loglogs[:, BLOCK : 2 * BLOCK], loglogs[:, 0:BLOCK])
 
         identity = held.tile([P, P], F32, name="identity")
         make_identity(nc, identity[:])

@@ -36,10 +36,10 @@ def tile_learnable_edge_pruning_kernel(tc, table, w_src, w_dst, b1, w2, u1, u2, 
 
         proj_src = held.tile([P, P], BF16, name="proj_src")
         nc.sync.dma_start(proj_src[:], w_src)
-        proj_dst = held.tile([P, P], BF16, name="proj_dst")
-        nc.sync.dma_start(proj_dst[:], w_dst)
         offsets = held.tile([P, 2 * EDGES // 16], U16, name="offsets")
         nc.sync.dma_start(offsets[:], offs)
+        proj_dst = held.tile([P, P], BF16, name="proj_dst")
+        nc.sync.dma_start(proj_dst[:], w_dst)
 
         draws = held.tile([P, 2 * BLOCK], F32, name="draws")
         nc.vector.memset(draws[:], 0.5)

@@ -10,24 +10,26 @@ NODES = 4096
 EDGES = 2048
 PIECE = 512
 PIECES = EDGES // PIECE
-BLOCK = 128
-BLOCKS_IN_PIECE = PIECE // BLOCK
 GROUP = 32
-ROW_STEP = GROUP // PIECES
+GROUPS = P // GROUP
+BLOCK = 64
+SPAN = GROUPS * BLOCK
+SPANS = EDGES // SPAN
+ROW_STEP = GROUP // SPANS
 B2 = 0.25
 
 FLOPS = 2 * P * P * 2 * EDGES + 2 * P * EDGES
 
 
 def by_block(row):
-    return row.rearrange("o (q k c) -> (o k) q c", q=PIECES, k=BLOCKS_IN_PIECE)
+    return row.rearrange("o (s g c) -> (o g) s c", s=SPANS, g=GROUPS)
 
 
 def tile_learnable_edge_pruning_kernel(tc, table, w_src, w_dst, b1, w2, u1, u2, offs, out):
     nc = tc.nc
     with (
         tc.tile_pool(name="held", bufs=1) as held,
-        tc.tile_pool(name="hidden", bufs=PIECES) as hidden,
+        tc.tile_pool(name="hidden", bufs=SPANS) as hidden,
         tc.psum_pool(name="banks", bufs=PIECES) as banks,
         tc.psum_pool(name="score", bufs=1) as score,
     ):
@@ -76,24 +78,29 @@ def tile_learnable_edge_pruning_kernel(tc, table, w_src, w_dst, b1, w2, u1, u2, 
                 bank[:], proj_dst[:], nodes[:].indirect(offsets[:, dst_col : dst_col + PIECE // 16]),
                 start=False, stop=True,
             )
-            h = hidden.tile([P, PIECE], BF16, name="h")
-            nc.vector.tensor_scalar(h[:], bank[:], bias1[:, 0:1], 0.0, op0=ALU.add, op1=ALU.max)
-            return h
+            h_of_spans = []
+            for edge in range(0, PIECE, SPAN):
+                h = hidden.tile([P, SPAN], BF16, name="h")
+                nc.vector.tensor_scalar(
+                    h[:], bank[:, edge : edge + SPAN], bias1[:, 0:1], 0.0, op0=ALU.add, op1=ALU.max
+                )
+                h_of_spans.append(h)
+            return h_of_spans
 
-        def second_layer(q, h):
-            row = ROW_STEP * q
-            for k in range(BLOCKS_IN_PIECE):
+        def second_layer(s, h):
+            row = ROW_STEP * s
+            for g in range(GROUPS):
                 nc.tensor.matmul(
-                    logits[GROUP * k : GROUP * (k + 1), :],
+                    logits[GROUP * g : GROUP * (g + 1), :],
                     w2_shift[:, GROUP - row : 2 * GROUP - row],
-                    h[:, k * BLOCK : (k + 1) * BLOCK],
-                    start=False, stop=(q == PIECES - 1),
+                    h[:, g * BLOCK : (g + 1) * BLOCK],
+                    start=False, stop=(s == SPANS - 1),
                 )
 
-        h_of = [first_layer(q) for q in range(PIECES)]
+        h_of = [h for q in range(PIECES) for h in first_layer(q)]
         nc.tensor.matmul(logits[:], identity[:], noise[:], start=True, stop=False)
-        for q in range(PIECES):
-            second_layer(q, h_of[q])
+        for s in range(SPANS):
+            second_layer(s, h_of[s])
 
         keep = held.tile([P, BLOCK], F32, name="keep")
         nc.scalar.activation(keep[:], logits[:], ACT.Sigmoid, bias=B2)

@@ -54,6 +54,11 @@ def tile_learnable_edge_pruning_kernel(tc, table, w_src, w_dst, b1, w2, u1, u2, 
         nc.vector.memset(w2_shift[:], 0.0)
         nc.gpsimd.dma_start(w2_shift[:, GROUP : GROUP + 1], w2)
 
+        ones = held.tile([P, 1], F32, name="ones")
+        nc.vector.memset(ones[:], 1.0)
+        log_of_ones = held.tile([P, 1], F32, name="log_of_ones")
+        nc.scalar.activation(log_of_ones[:], ones[:], ACT.Ln)
+
         logs = held.tile([P, 2 * BLOCK], F32, name="logs")
         nc.scalar.activation(logs[:], draws[:], ACT.Ln)
         loglogs = held.tile([P, 2 * BLOCK], F32, name="loglogs")

import concourse.mybir as mybir
from concourse.masks import make_identity

BF16, F32, U16 = mybir.dt.bfloat16, mybir.dt.float32, mybir.dt.uint16
ACT = mybir.ActivationFunctionType
ALU = mybir.AluOpType

P = 128
NODES = 4096
EDGES = 2048
PIECE = 512
PIECES = EDGES // PIECE
GROUP = 32
GROUPS = P // GROUP
BLOCK = 64
SPAN = GROUPS * BLOCK
SPANS = EDGES // SPAN
ROW_STEP = GROUP // SPANS
B2 = 0.25

FLOPS = 2 * P * P * 2 * EDGES + 2 * P * EDGES


def by_block(row):
    return row.rearrange("o (s g c) -> (o g) s c", s=SPANS, g=GROUPS)


def tile_learnable_edge_pruning_kernel(tc, table, w_src, w_dst, b1, w2, u1, u2, offs, out):
    nc = tc.nc
    with (
        tc.tile_pool(name="held", bufs=1) as held,
        tc.tile_pool(name="hidden", bufs=SPANS) as hidden,
        tc.psum_pool(name="banks", bufs=PIECES) as banks,
        tc.psum_pool(name="score", bufs=1) as score,
    ):
        nodes = held.tile([P, NODES], BF16, name="nodes")
        nc.scalar.dma_start(nodes[:], table)

        proj_src = held.tile([P, P], BF16, name="proj_src")
        nc.sync.dma_start(proj_src[:], w_src)
        offsets = held.tile([P, 2 * EDGES // 16], U16, name="offsets")
        nc.sync.dma_start(offsets[:], offs)
        proj_dst = held.tile([P, P], BF16, name="proj_dst")
        nc.sync.dma_start(proj_dst[:], w_dst)

        draws = held.tile([P, 2 * BLOCK], F32, name="draws")
        nc.vector.memset(draws[:], 0.5)
        nc.scalar.dma_start(draws[0:P:ROW_STEP, 0:BLOCK], by_block(u1))
        nc.scalar.dma_start(draws[0:P:ROW_STEP, BLOCK : 2 * BLOCK], by_block(u2))
        bias1 = held.tile([P, 1], F32, name="bias1")
        nc.gpsimd.dma_start(bias1[:], b1)

        w2_shift = held.tile([P, 2 * GROUP], BF16, name="w2_shift")
        nc.vector.memset(w2_shift[:], 0.0)
        nc.gpsimd.dma_start(w2_shift[:, GROUP : GROUP + 1], w2)

        ones = held.tile([P, 1], F32, name="ones")
        nc.vector.memset(ones[:], 1.0)
        log_of_ones = held.tile([P, 1], F32, name="log_of_ones")
        nc.scalar.activation(log_of_ones[:], ones[:], ACT.Ln)

        logs = held.tile([P, 2 * BLOCK], F32, name="logs")
        nc.scalar.activation(logs[:], draws[:], ACT.Ln)
        loglogs = held.tile([P, 2 * BLOCK], F32, name="loglogs")
        nc.scalar.activation(loglogs[:], logs[:], ACT.Ln, scale=-1.0)
        noise = held.tile([P, BLOCK], F32, name="noise")
        nc.gpsimd.tensor_sub(noise[:], loglogs[:, BLOCK : 2 * BLOCK], loglogs[:, 0:BLOCK])

        identity = held.tile([P, P], F32, name="identity")
        make_identity(nc, identity[:])

        logits = score.tile([P, BLOCK], F32, name="logits")

        def first_layer(q):
            bank = banks.tile([P, PIECE], F32, name="bank")
            src_col = q * PIECE // 16
            dst_col = (EDGES + q * PIECE) // 16
            nc.tensor.matmul(
                bank[:], proj_src[:], nodes[:].indirect(offsets[:, src_col : src_col + PIECE // 16]),
                start=True, stop=False,
            )
            nc.tensor.matmul(
                bank[:], proj_dst[:], nodes[:].indirect(offsets[:, dst_col : dst_col + PIECE // 16]),
                start=False, stop=True,
            )
            h_of_spans = []
            for edge in range(0, PIECE, SPAN):
                h = hidden.tile([P, SPAN], BF16, name="h")
                nc.vector.tensor_scalar(
                    h[:], bank[:, edge : edge + SPAN], bias1[:, 0:1], 0.0, op0=ALU.add, op1=ALU.max
                )
                h_of_spans.append(h)
            return h_of_spans

        def second_layer(s, h):
            row = ROW_STEP * s
            for g in range(GROUPS):
                nc.tensor.matmul(
                    logits[GROUP * g : GROUP * (g + 1), :],
                    w2_shift[:, GROUP - row : 2 * GROUP - row],
                    h[:, g * BLOCK : (g + 1) * BLOCK],
                    start=False, stop=(s == SPANS - 1),
                )

        h_of = [h for q in range(PIECES) for h in first_layer(q)]
        nc.tensor.matmul(logits[:], identity[:], noise[:], start=True, stop=False)
        for s in range(SPANS):
            second_layer(s, h_of[s])

        keep = held.tile([P, BLOCK], F32, name="keep")
        nc.scalar.activation(keep[:], logits[:], ACT.Sigmoid, bias=B2)
        nc.sync.dma_start(by_block(out), keep[0:P:ROW_STEP, :])
